import numpy as np
import ml_dtypes

BF16 = ml_dtypes.bfloat16


def bf(x):
    return np.asarray(x, np.float32).astype(BF16)


def f32(x):
    return np.asarray(x, np.float32)


def f64(x):
    return np.asarray(x).astype(np.float64)


def striped(idx):
    return np.tile(idx.reshape(-1, 16).T, (8, 1))


C, S, N, K = 128, 1024, 512, 7


def setup_inputs():
    return {"x": f32(np.random.uniform(0.0, 1.0, (C, S))), "y": f32(np.random.uniform(0.0, 1.0, (C, N))), "theta": f32(np.random.uniform(-1.5, 1.5, (1, K))), "offs": striped(np.random.permutation(np.tile(np.arange(S), 2))[:N])}


def reference(x, y, theta, offs):
    idx = offs[:16].T.reshape(-1)
    cw, sw = np.cos(0.5 * f64(x)), np.sin(0.5 * f64(x))
    cb, sb = np.cos(0.5 * f64(y)), np.sin(0.5 * f64(y))
    amp0 = cw[:, idx] * cb
    amp1 = cw[:, idx] * sb
    amp2 = sw[:, idx] * sb
    amp3 = sw[:, idx] * cb
    ct, st = np.cos(0.5 * f64(theta))[0], np.sin(0.5 * f64(theta))[0]
    blocks = []
    for t in range(K):
        n0 = ct[t] * amp0 - st[t] * amp2
        n2 = st[t] * amp0 + ct[t] * amp2
        n1 = ct[t] * amp1 - st[t] * amp3
        n3 = st[t] * amp1 + ct[t] * amp3
        p0, p1, p2, p3 = n0 * n0, n1 * n1, n2 * n2, n3 * n3
        blocks.append((p0 + p1 - p2 - p3 + 1.0) * 0.5)
        blocks.append((p0 - p1 + p2 - p3 + 1.0) * 0.5)
    return np.concatenate(blocks, axis=1)

@@ -1,0 +1,98 @@
+import math
+
+import concourse.mybir as mybir
+
+F32 = mybir.dt.float32
+I32 = mybir.dt.int32
+U16 = mybir.dt.uint16
+ALU = mybir.AluOpType
+FUNC = mybir.ActivationFunctionType
+
+IMAGES = 128
+PIXELS = 1024
+PAIRS = 512
+CLASSES = 7
+TWO_PI = 2.0 * math.pi
+
+
+def wrap_angle(nc, pool, angle, width, name):
+    turns = pool.tile([IMAGES, width], I32, name=name + "_turns")
+    nc.vector.tensor_scalar(turns[:], angle[:], 1.0 / TWO_PI, None, ALU.mult)
+    wrapped = pool.tile([IMAGES, width], F32, name=name + "_wrapped")
+    nc.vector.scalar_tensor_tensor(wrapped[:], turns[:], -TWO_PI, angle[:], ALU.mult, ALU.add)
+    return wrapped
+
+
+def tile_jointmembership_fuzzylayer_jaffe_nopool_kernel(tc, x, y, theta, offs, out):
+    nc = tc.nc
+    with tc.tile_pool(name="held", bufs=1) as held:
+        offsets = held.tile([IMAGES, PAIRS // 16], U16, name="offsets")
+        nc.sync.dma_start(offsets[:], offs)
+        theta_all = held.tile([IMAGES, CLASSES], F32, name="theta_all")
+        nc.sync.dma_start(theta_all[:], theta.broadcast_to([IMAGES, CLASSES]))
+        y_in = held.tile([IMAGES, PAIRS], F32, name="y_in")
+        nc.sync.dma_start(y_in[:], y)
+        x_in = held.tile([IMAGES, PIXELS], F32, name="x_in")
+        nc.sync.dma_start(x_in[:], x)
+
+        half_pi = held.tile([IMAGES, 1], F32, name="half_pi")
+        nc.vector.memset(half_pi[:], 0.5 * math.pi)
+
+        theta_wrapped = wrap_angle(nc, held, theta_all, CLASSES, "theta")
+        sin_theta = held.tile([IMAGES, CLASSES], F32, name="sin_theta")
+        nc.scalar.activation(sin_theta[:], theta_wrapped[:], FUNC.Sin)
+        st = held.tile([IMAGES, CLASSES], F32, name="st")
+        nc.scalar.activation(st[:], theta_wrapped[:], FUNC.Sin, scale=0.5)
+        minus_2_sin_theta = held.tile([IMAGES, CLASSES], F32, name="minus_2_sin_theta")
+        nc.vector.tensor_scalar(minus_2_sin_theta[:], sin_theta[:], -2.0, None, ALU.mult)
+        st_squared = held.tile([IMAGES, CLASSES], F32, name="st_squared")
+        nc.vector.tensor_tensor(st_squared[:], st[:], st[:], ALU.mult)
+        cos_theta = held.tile([IMAGES, CLASSES], F32, name="cos_theta")
+        nc.vector.tensor_scalar(cos_theta[:], st_squared[:], -2.0, 1.0, ALU.mult, ALU.add)
+
+        y_wrapped = wrap_angle(nc, held, y_in, PAIRS, "y")
+        sb = held.tile([IMAGES, PAIRS], F32, name="sb")
+        nc.scalar.activation(sb[:], y_wrapped[:], FUNC.Sin, scale=0.5)
+        cb = held.tile([IMAGES, PAIRS], F32, name="cb")
+        nc.scalar.activation(cb[:], y_wrapped[:], FUNC.Sin, bias=half_pi[:], scale=0.5)
+        sb_squared = held.tile([IMAGES, PAIRS], F32, name="sb_squared")
+        nc.scalar.activation(sb_squared[:], sb[:], FUNC.Square)
+
+        x_wrapped = wrap_angle(nc, held, x_in, PIXELS, "x")
+        sa_all = held.tile([IMAGES, PIXELS], F32, name="sa_all")
+        nc.scalar.activation(sa_all[:], x_wrapped[:], FUNC.Sin, scale=0.5)
+        ca_all = held.tile([IMAGES, PIXELS], F32, name="ca_all")
+        nc.scalar.activation(ca_all[:], x_wrapped[:], FUNC.Sin, bias=half_pi[:], scale=0.5)
+
+        amp2 = held.tile([IMAGES, PAIRS], F32, name="amp2")
+        nc.vector.tensor_tensor(amp2[:], sa_all[:].indirect(offsets[:]), sb[:], ALU.mult)
+        amp0 = held.tile([IMAGES, PAIRS], F32, name="amp0")
+        nc.vector.tensor_tensor(amp0[:], ca_all[:].indirect(offsets[:]), cb[:], ALU.mult)
+
+        amp2_squared = held.tile([IMAGES, PAIRS], F32, name="amp2_squared")
+        nc.scalar.activation(amp2_squared[:], amp2[:], FUNC.Square)
+        amp0_squared = held.tile([IMAGES, PAIRS], F32, name="amp0_squared")
+        nc.scalar.activation(amp0_squared[:], amp0[:], FUNC.Square)
+
+        odd_block = held.tile([IMAGES, PAIRS], F32, name="odd_block")
+        nc.vector.tensor_tensor(odd_block[:], amp0_squared[:], amp2_squared[:], ALU.add)
+        for t in range(CLASSES):
+            nc.sync.dma_start(out[:, (2 * t + 1) * PAIRS : (2 * t + 2) * PAIRS], odd_block[:])
+
+        amp1_squared = held.tile([IMAGES, PAIRS], F32, name="amp1_squared")
+        nc.vector.tensor_tensor(amp1_squared[:], sb_squared[:], amp2_squared[:], ALU.subtract)
+        ca_squared = held.tile([IMAGES, PAIRS], F32, name="ca_squared")
+        nc.vector.tensor_tensor(ca_squared[:], amp0_squared[:], amp1_squared[:], ALU.add)
+        amp0_amp2 = held.tile([IMAGES, PAIRS], F32, name="amp0_amp2")
+        nc.vector.tensor_tensor(amp0_amp2[:], amp0[:], amp2[:], ALU.mult)
+        for t in range(CLASSES):
+            ca_term = held.tile([IMAGES, PAIRS], F32, name=f"ca_term{t}")
+            nc.scalar.activation(
+                ca_term[:], ca_squared[:], FUNC.Identity,
+                bias=st_squared[:, t : t + 1], scale=cos_theta[:, t : t + 1],
+            )
+            even_block = held.tile([IMAGES, PAIRS], F32, name=f"even_block{t}")
+            nc.vector.scalar_tensor_tensor(
+                even_block[:], amp0_amp2[:], minus_2_sin_theta[:, t : t + 1], ca_term[:], ALU.mult, ALU.add
+            )
+            nc.sync.dma_start(out[:, 2 * t * PAIRS : (2 * t + 1) * PAIRS], even_block[:])

@@ -13,6 +13,8 @@ PIXELS = 1024
 PAIRS = 512
 CLASSES = 7
 TWO_PI = 2.0 * math.pi
+X_PIECES = 4
+PIECE = PIXELS // X_PIECES
 
 
 def wrap_angle(nc, pool, angle, width, name):
@@ -29,11 +31,14 @@ def tile_jointmembership_fuzzylayer_jaffe_nopool_kernel(tc, x, y, theta, offs, o
         offsets = held.tile([IMAGES, PAIRS // 16], U16, name="offsets")
         nc.sync.dma_start(offsets[:], offs)
         theta_all = held.tile([IMAGES, CLASSES], F32, name="theta_all")
-        nc.sync.dma_start(theta_all[:], theta.broadcast_to([IMAGES, CLASSES]))
+        nc.scalar.dma_start(theta_all[:], theta.broadcast_to([IMAGES, CLASSES]))
         y_in = held.tile([IMAGES, PAIRS], F32, name="y_in")
-        nc.sync.dma_start(y_in[:], y)
-        x_in = held.tile([IMAGES, PIXELS], F32, name="x_in")
-        nc.sync.dma_start(x_in[:], x)
+        nc.scalar.dma_start(y_in[:], y)
+        x_pieces = []
+        for p in range(X_PIECES):
+            x_piece = held.tile([IMAGES, PIECE], F32, name=f"x_piece{p}")
+            nc.sync.dma_start(x_piece[:], x[:, p * PIECE : (p + 1) * PIECE])
+            x_pieces.append(x_piece)
 
         half_pi = held.tile([IMAGES, 1], F32, name="half_pi")
         nc.vector.memset(half_pi[:], 0.5 * math.pi)
@@ -53,34 +58,39 @@ def tile_jointmembership_fuzzylayer_jaffe_nopool_kernel(tc, x, y, theta, offs, o
         y_wrapped = wrap_angle(nc, held, y_in, PAIRS, "y")
         sb = held.tile([IMAGES, PAIRS], F32, name="sb")
         nc.scalar.activation(sb[:], y_wrapped[:], FUNC.Sin, scale=0.5)
-        cb = held.tile([IMAGES, PAIRS], F32, name="cb")
-        nc.scalar.activation(cb[:], y_wrapped[:], FUNC.Sin, bias=half_pi[:], scale=0.5)
-        sb_squared = held.tile([IMAGES, PAIRS], F32, name="sb_squared")
-        nc.scalar.activation(sb_squared[:], sb[:], FUNC.Square)
-
-        x_wrapped = wrap_angle(nc, held, x_in, PIXELS, "x")
         sa_all = held.tile([IMAGES, PIXELS], F32, name="sa_all")
-        nc.scalar.activation(sa_all[:], x_wrapped[:], FUNC.Sin, scale=0.5)
-        ca_all = held.tile([IMAGES, PIXELS], F32, name="ca_all")
-        nc.scalar.activation(ca_all[:], x_wrapped[:], FUNC.Sin, bias=half_pi[:], scale=0.5)
-
+        x_wrapped = []
+        for p in range(X_PIECES):
+            x_wrapped.append(wrap_angle(nc, held, x_pieces[p], PIECE, f"x{p}"))
+            nc.scalar.activation(sa_all[:, p * PIECE : (p + 1) * PIECE], x_wrapped[p][:], FUNC.Sin, scale=0.5)
         amp2 = held.tile([IMAGES, PAIRS], F32, name="amp2")
         nc.vector.tensor_tensor(amp2[:], sa_all[:].indirect(offsets[:]), sb[:], ALU.mult)
+
+        cb = held.tile([IMAGES, PAIRS], F32, name="cb")
+        nc.scalar.activation(cb[:], y_wrapped[:], FUNC.Sin, bias=half_pi[:], scale=0.5)
+        ca_all = held.tile([IMAGES, PIXELS], F32, name="ca_all")
+        for p in range(X_PIECES):
+            nc.scalar.activation(
+                ca_all[:, p * PIECE : (p + 1) * PIECE], x_wrapped[p][:], FUNC.Sin, bias=half_pi[:], scale=0.5
+            )
         amp0 = held.tile([IMAGES, PAIRS], F32, name="amp0")
         nc.vector.tensor_tensor(amp0[:], ca_all[:].indirect(offsets[:]), cb[:], ALU.mult)
 
         amp2_squared = held.tile([IMAGES, PAIRS], F32, name="amp2_squared")
         nc.scalar.activation(amp2_squared[:], amp2[:], FUNC.Square)
+        sb_squared = held.tile([IMAGES, PAIRS], F32, name="sb_squared")
+        nc.scalar.activation(sb_squared[:], sb[:], FUNC.Square)
         amp0_squared = held.tile([IMAGES, PAIRS], F32, name="amp0_squared")
         nc.scalar.activation(amp0_squared[:], amp0[:], FUNC.Square)
+
+        amp1_squared = held.tile([IMAGES, PAIRS], F32, name="amp1_squared")
+        nc.vector.tensor_tensor(amp1_squared[:], sb_squared[:], amp2_squared[:], ALU.subtract)
 
         odd_block = held.tile([IMAGES, PAIRS], F32, name="odd_block")
         nc.vector.tensor_tensor(odd_block[:], amp0_squared[:], amp2_squared[:], ALU.add)
         for t in range(CLASSES):
             nc.sync.dma_start(out[:, (2 * t + 1) * PAIRS : (2 * t + 2) * PAIRS], odd_block[:])
 
-        amp1_squared = held.tile([IMAGES, PAIRS], F32, name="amp1_squared")
-        nc.vector.tensor_tensor(amp1_squared[:], sb_squared[:], amp2_squared[:], ALU.subtract)
         ca_squared = held.tile([IMAGES, PAIRS], F32, name="ca_squared")
         nc.vector.tensor_tensor(ca_squared[:], amp0_squared[:], amp1_squared[:], ALU.add)
         amp0_amp2 = held.tile([IMAGES, PAIRS], F32, name="amp0_amp2")

@@ -13,8 +13,26 @@ PIXELS = 1024
 PAIRS = 512
 CLASSES = 7
 TWO_PI = 2.0 * math.pi
-X_PIECES = 4
-PIECE = PIXELS // X_PIECES
+PIECE = 256
+HALF = PAIRS // 2
+
+
+def load_and_wrap(nc, pool, source, width, name):
+    wrapped_pieces = []
+    for p in range(width // PIECE):
+        piece = pool.tile([IMAGES, PIECE], F32, name=f"{name}{p}")
+        nc.sync.dma_start(piece[:], source[:, p * PIECE : (p + 1) * PIECE])
+        wrapped_pieces.append(wrap_angle(nc, pool, piece, PIECE, f"{name}{p}"))
+    return wrapped_pieces
+
+
+def sin_of_half(nc, result, wrapped_pieces, shift):
+    for p, wrapped in enumerate(wrapped_pieces):
+        columns = result[:, p * PIECE : (p + 1) * PIECE]
+        if shift is None:
+            nc.scalar.activation(columns, wrapped[:], FUNC.Sin, scale=0.5)
+        else:
+            nc.scalar.activation(columns, wrapped[:], FUNC.Sin, bias=shift[:], scale=0.5)
 
 
 def wrap_angle(nc, pool, angle, width, name):
@@ -28,26 +46,50 @@ def wrap_angle(nc, pool, angle, width, name):
 def tile_jointmembership_fuzzylayer_jaffe_nopool_kernel(tc, x, y, theta, offs, out):
     nc = tc.nc
     with tc.tile_pool(name="held", bufs=1) as held:
-        offsets = held.tile([IMAGES, PAIRS // 16], U16, name="offsets")
-        nc.sync.dma_start(offsets[:], offs)
-        theta_all = held.tile([IMAGES, CLASSES], F32, name="theta_all")
-        nc.scalar.dma_start(theta_all[:], theta.broadcast_to([IMAGES, CLASSES]))
-        y_in = held.tile([IMAGES, PAIRS], F32, name="y_in")
-        nc.scalar.dma_start(y_in[:], y)
-        x_pieces = []
-        for p in range(X_PIECES):
-            x_piece = held.tile([IMAGES, PIECE], F32, name=f"x_piece{p}")
-            nc.sync.dma_start(x_piece[:], x[:, p * PIECE : (p + 1) * PIECE])
-            x_pieces.append(x_piece)
-
         half_pi = held.tile([IMAGES, 1], F32, name="half_pi")
         nc.vector.memset(half_pi[:], 0.5 * math.pi)
 
+        theta_all = held.tile([IMAGES, CLASSES], F32, name="theta_all")
+        nc.scalar.dma_start(theta_all[:], theta.broadcast_to([IMAGES, CLASSES]))
         theta_wrapped = wrap_angle(nc, held, theta_all, CLASSES, "theta")
         sin_theta = held.tile([IMAGES, CLASSES], F32, name="sin_theta")
         nc.scalar.activation(sin_theta[:], theta_wrapped[:], FUNC.Sin)
         st = held.tile([IMAGES, CLASSES], F32, name="st")
         nc.scalar.activation(st[:], theta_wrapped[:], FUNC.Sin, scale=0.5)
+
+        y_wrapped = load_and_wrap(nc, held, y, PAIRS, "y")
+        x_wrapped = load_and_wrap(nc, held, x, PIXELS, "x")
+        offsets = held.tile([IMAGES, PAIRS // 16], U16, name="offsets")
+        nc.sync.dma_start(offsets[:], offs)
+
+        sb = held.tile([IMAGES, PAIRS], F32, name="sb")
+        sin_of_half(nc, sb, y_wrapped, None)
+        sa_all = held.tile([IMAGES, PIXELS], F32, name="sa_all")
+        sin_of_half(nc, sa_all, x_wrapped, None)
+        amp2 = held.tile([IMAGES, PAIRS], F32, name="amp2")
+        nc.vector.tensor_tensor(amp2[:], sa_all[:].indirect(offsets[:]), sb[:], ALU.mult)
+
+        cb = held.tile([IMAGES, PAIRS], F32, name="cb")
+        sin_of_half(nc, cb, y_wrapped, half_pi)
+        ca_all = held.tile([IMAGES, PIXELS], F32, name="ca_all")
+        sin_of_half(nc, ca_all, x_wrapped, half_pi)
+        amp2_squared = held.tile([IMAGES, PAIRS], F32, name="amp2_squared")
+        nc.scalar.activation(amp2_squared[:], amp2[:], FUNC.Square)
+
+        amp0 = held.tile([IMAGES, PAIRS], F32, name="amp0")
+        amp0_squared = held.tile([IMAGES, PAIRS], F32, name="amp0_squared")
+        odd_block = held.tile([IMAGES, PAIRS], F32, name="odd_block")
+        for h in range(2):
+            half = slice(h * HALF, (h + 1) * HALF)
+            half_of_list = offsets[:, h * HALF // 16 : (h + 1) * HALF // 16]
+            nc.vector.tensor_tensor(amp0[:, half], ca_all[:].indirect(half_of_list), cb[:, half], ALU.mult)
+            nc.scalar.activation(amp0_squared[:, half], amp0[:, half], FUNC.Square)
+        for h in range(2):
+            half = slice(h * HALF, (h + 1) * HALF)
+            nc.vector.tensor_tensor(odd_block[:, half], amp0_squared[:, half], amp2_squared[:, half], ALU.add)
+        for t in range(CLASSES):
+            nc.sync.dma_start(out[:, (2 * t + 1) * PAIRS : (2 * t + 2) * PAIRS], odd_block[:])
+
         minus_2_sin_theta = held.tile([IMAGES, CLASSES], F32, name="minus_2_sin_theta")
         nc.vector.tensor_scalar(minus_2_sin_theta[:], sin_theta[:], -2.0, None, ALU.mult)
         st_squared = held.tile([IMAGES, CLASSES], F32, name="st_squared")
@@ -55,42 +97,10 @@ def tile_jointmembership_fuzzylayer_jaffe_nopool_kernel(tc, x, y, theta, offs, o
         cos_theta = held.tile([IMAGES, CLASSES], F32, name="cos_theta")
         nc.vector.tensor_scalar(cos_theta[:], st_squared[:], -2.0, 1.0, ALU.mult, ALU.add)
 
-        y_wrapped = wrap_angle(nc, held, y_in, PAIRS, "y")
-        sb = held.tile([IMAGES, PAIRS], F32, name="sb")
-        nc.scalar.activation(sb[:], y_wrapped[:], FUNC.Sin, scale=0.5)
-        sa_all = held.tile([IMAGES, PIXELS], F32, name="sa_all")
-        x_wrapped = []
-        for p in range(X_PIECES):
-            x_wrapped.append(wrap_angle(nc, held, x_pieces[p], PIECE, f"x{p}"))
-            nc.scalar.activation(sa_all[:, p * PIECE : (p + 1) * PIECE], x_wrapped[p][:], FUNC.Sin, scale=0.5)
-        amp2 = held.tile([IMAGES, PAIRS], F32, name="amp2")
-        nc.vector.tensor_tensor(amp2[:], sa_all[:].indirect(offsets[:]), sb[:], ALU.mult)
-
-        cb = held.tile([IMAGES, PAIRS], F32, name="cb")
-        nc.scalar.activation(cb[:], y_wrapped[:], FUNC.Sin, bias=half_pi[:], scale=0.5)
-        ca_all = held.tile([IMAGES, PIXELS], F32, name="ca_all")
-        for p in range(X_PIECES):
-            nc.scalar.activation(
-                ca_all[:, p * PIECE : (p + 1) * PIECE], x_wrapped[p][:], FUNC.Sin, bias=half_pi[:], scale=0.5
-            )
-        amp0 = held.tile([IMAGES, PAIRS], F32, name="amp0")
-        nc.vector.tensor_tensor(amp0[:], ca_all[:].indirect(offsets[:]), cb[:], ALU.mult)
-
-        amp2_squared = held.tile([IMAGES, PAIRS], F32, name="amp2_squared")
-        nc.scalar.activation(amp2_squared[:], amp2[:], FUNC.Square)
         sb_squared = held.tile([IMAGES, PAIRS], F32, name="sb_squared")
         nc.scalar.activation(sb_squared[:], sb[:], FUNC.Square)
-        amp0_squared = held.tile([IMAGES, PAIRS], F32, name="amp0_squared")
-        nc.scalar.activation(amp0_squared[:], amp0[:], FUNC.Square)
-
         amp1_squared = held.tile([IMAGES, PAIRS], F32, name="amp1_squared")
         nc.vector.tensor_tensor(amp1_squared[:], sb_squared[:], amp2_squared[:], ALU.subtract)
-
-        odd_block = held.tile([IMAGES, PAIRS], F32, name="odd_block")
-        nc.vector.tensor_tensor(odd_block[:], amp0_squared[:], amp2_squared[:], ALU.add)
-        for t in range(CLASSES):
-            nc.sync.dma_start(out[:, (2 * t + 1) * PAIRS : (2 * t + 2) * PAIRS], odd_block[:])
-
         ca_squared = held.tile([IMAGES, PAIRS], F32, name="ca_squared")
         nc.vector.tensor_tensor(ca_squared[:], amp0_squared[:], amp1_squared[:], ALU.add)
         amp0_amp2 = held.tile([IMAGES, PAIRS], F32, name="amp0_amp2")

@@ -13,34 +13,30 @@ PIXELS = 1024
 PAIRS = 512
 CLASSES = 7
 TWO_PI = 2.0 * math.pi
-PIECE = 256
+PIECE = 512
 HALF = PAIRS // 2
 
 
-def load_and_wrap(nc, pool, source, width, name):
-    wrapped_pieces = []
-    for p in range(width // PIECE):
-        piece = pool.tile([IMAGES, PIECE], F32, name=f"{name}{p}")
-        nc.sync.dma_start(piece[:], source[:, p * PIECE : (p + 1) * PIECE])
-        wrapped_pieces.append(wrap_angle(nc, pool, piece, PIECE, f"{name}{p}"))
-    return wrapped_pieces
-
-
-def sin_of_half(nc, result, wrapped_pieces, shift):
-    for p, wrapped in enumerate(wrapped_pieces):
-        columns = result[:, p * PIECE : (p + 1) * PIECE]
-        if shift is None:
-            nc.scalar.activation(columns, wrapped[:], FUNC.Sin, scale=0.5)
-        else:
-            nc.scalar.activation(columns, wrapped[:], FUNC.Sin, bias=shift[:], scale=0.5)
-
-
 def wrap_angle(nc, pool, angle, width, name):
+    pieces = [slice(first, min(first + PIECE, width)) for first in range(0, width, PIECE)]
     turns = pool.tile([IMAGES, width], I32, name=name + "_turns")
-    nc.vector.tensor_scalar(turns[:], angle[:], 1.0 / TWO_PI, None, ALU.mult)
+    for piece in pieces:
+        nc.vector.tensor_scalar(turns[:, piece], angle[:, piece], 1.0 / TWO_PI, None, ALU.mult)
     wrapped = pool.tile([IMAGES, width], F32, name=name + "_wrapped")
-    nc.vector.scalar_tensor_tensor(wrapped[:], turns[:], -TWO_PI, angle[:], ALU.mult, ALU.add)
+    for piece in pieces:
+        nc.vector.scalar_tensor_tensor(
+            wrapped[:, piece], turns[:, piece], -TWO_PI, angle[:, piece], ALU.mult, ALU.add
+        )
     return wrapped
+
+
+def sin_of_half(nc, result, wrapped, width, shift):
+    for first in range(0, width, PIECE):
+        piece = slice(first, first + PIECE)
+        if shift is None:
+            nc.scalar.activation(result[:, piece], wrapped[:, piece], FUNC.Sin, scale=0.5)
+        else:
+            nc.scalar.activation(result[:, piece], wrapped[:, piece], FUNC.Sin, bias=shift[:], scale=0.5)
 
 
 def tile_jointmembership_fuzzylayer_jaffe_nopool_kernel(tc, x, y, theta, offs, out):
@@ -57,22 +53,26 @@ def tile_jointmembership_fuzzylayer_jaffe_nopool_kernel(tc, x, y, theta, offs, o
         st = held.tile([IMAGES, CLASSES], F32, name="st")
         nc.scalar.activation(st[:], theta_wrapped[:], FUNC.Sin, scale=0.5)
 
-        y_wrapped = load_and_wrap(nc, held, y, PAIRS, "y")
-        x_wrapped = load_and_wrap(nc, held, x, PIXELS, "x")
+        y_in = held.tile([IMAGES, PAIRS], F32, name="y_in")
+        nc.sync.dma_start(y_in[:], y)
+        x_in = held.tile([IMAGES, PIXELS], F32, name="x_in")
+        nc.sync.dma_start(x_in[:], x)
         offsets = held.tile([IMAGES, PAIRS // 16], U16, name="offsets")
         nc.sync.dma_start(offsets[:], offs)
+        y_wrapped = wrap_angle(nc, held, y_in, PAIRS, "y")
+        x_wrapped = wrap_angle(nc, held, x_in, PIXELS, "x")
 
         sb = held.tile([IMAGES, PAIRS], F32, name="sb")
-        sin_of_half(nc, sb, y_wrapped, None)
+        sin_of_half(nc, sb, y_wrapped, PAIRS, None)
         sa_all = held.tile([IMAGES, PIXELS], F32, name="sa_all")
-        sin_of_half(nc, sa_all, x_wrapped, None)
+        sin_of_half(nc, sa_all, x_wrapped, PIXELS, None)
         amp2 = held.tile([IMAGES, PAIRS], F32, name="amp2")
         nc.vector.tensor_tensor(amp2[:], sa_all[:].indirect(offsets[:]), sb[:], ALU.mult)
 
         cb = held.tile([IMAGES, PAIRS], F32, name="cb")
-        sin_of_half(nc, cb, y_wrapped, half_pi)
+        sin_of_half(nc, cb, y_wrapped, PAIRS, half_pi)
         ca_all = held.tile([IMAGES, PIXELS], F32, name="ca_all")
-        sin_of_half(nc, ca_all, x_wrapped, half_pi)
+        sin_of_half(nc, ca_all, x_wrapped, PIXELS, half_pi)
         amp2_squared = held.tile([IMAGES, PAIRS], F32, name="amp2_squared")
         nc.scalar.activation(amp2_squared[:], amp2[:], FUNC.Square)
 

@@ -13,7 +13,7 @@ PIXELS = 1024
 PAIRS = 512
 CLASSES = 7
 TWO_PI = 2.0 * math.pi
-PIECE = 512
+PIECE = 256
 HALF = PAIRS // 2
 
 
@@ -45,22 +45,17 @@ def tile_jointmembership_fuzzylayer_jaffe_nopool_kernel(tc, x, y, theta, offs, o
         half_pi = held.tile([IMAGES, 1], F32, name="half_pi")
         nc.vector.memset(half_pi[:], 0.5 * math.pi)
 
-        theta_all = held.tile([IMAGES, CLASSES], F32, name="theta_all")
-        nc.scalar.dma_start(theta_all[:], theta.broadcast_to([IMAGES, CLASSES]))
-        theta_wrapped = wrap_angle(nc, held, theta_all, CLASSES, "theta")
-        sin_theta = held.tile([IMAGES, CLASSES], F32, name="sin_theta")
-        nc.scalar.activation(sin_theta[:], theta_wrapped[:], FUNC.Sin)
-        st = held.tile([IMAGES, CLASSES], F32, name="st")
-        nc.scalar.activation(st[:], theta_wrapped[:], FUNC.Sin, scale=0.5)
-
         y_in = held.tile([IMAGES, PAIRS], F32, name="y_in")
         nc.sync.dma_start(y_in[:], y)
         x_in = held.tile([IMAGES, PIXELS], F32, name="x_in")
         nc.sync.dma_start(x_in[:], x)
         offsets = held.tile([IMAGES, PAIRS // 16], U16, name="offsets")
         nc.sync.dma_start(offsets[:], offs)
+        theta_all = held.tile([IMAGES, CLASSES], F32, name="theta_all")
+        nc.sync.dma_start(theta_all[:], theta.broadcast_to([IMAGES, CLASSES]))
         y_wrapped = wrap_angle(nc, held, y_in, PAIRS, "y")
         x_wrapped = wrap_angle(nc, held, x_in, PIXELS, "x")
+        theta_wrapped = wrap_angle(nc, held, theta_all, CLASSES, "theta")
 
         sb = held.tile([IMAGES, PAIRS], F32, name="sb")
         sin_of_half(nc, sb, y_wrapped, PAIRS, None)
@@ -90,6 +85,10 @@ def tile_jointmembership_fuzzylayer_jaffe_nopool_kernel(tc, x, y, theta, offs, o
         for t in range(CLASSES):
             nc.sync.dma_start(out[:, (2 * t + 1) * PAIRS : (2 * t + 2) * PAIRS], odd_block[:])
 
+        sin_theta = held.tile([IMAGES, CLASSES], F32, name="sin_theta")
+        nc.scalar.activation(sin_theta[:], theta_wrapped[:], FUNC.Sin)
+        st = held.tile([IMAGES, CLASSES], F32, name="st")
+        nc.scalar.activation(st[:], theta_wrapped[:], FUNC.Sin, scale=0.5)
         minus_2_sin_theta = held.tile([IMAGES, CLASSES], F32, name="minus_2_sin_theta")
         nc.vector.tensor_scalar(minus_2_sin_theta[:], sin_theta[:], -2.0, None, ALU.mult)
         st_squared = held.tile([IMAGES, CLASSES], F32, name="st_squared")

@@ -3,7 +3,6 @@ import math
 import concourse.mybir as mybir
 
 F32 = mybir.dt.float32
-I32 = mybir.dt.int32
 U16 = mybir.dt.uint16
 ALU = mybir.AluOpType
 FUNC = mybir.ActivationFunctionType
@@ -12,31 +11,7 @@ IMAGES = 128
 PIXELS = 1024
 PAIRS = 512
 CLASSES = 7
-TWO_PI = 2.0 * math.pi
-PIECE = 256
 HALF = PAIRS // 2
-
-
-def wrap_angle(nc, pool, angle, width, name):
-    pieces = [slice(first, min(first + PIECE, width)) for first in range(0, width, PIECE)]
-    turns = pool.tile([IMAGES, width], I32, name=name + "_turns")
-    for piece in pieces:
-        nc.vector.tensor_scalar(turns[:, piece], angle[:, piece], 1.0 / TWO_PI, None, ALU.mult)
-    wrapped = pool.tile([IMAGES, width], F32, name=name + "_wrapped")
-    for piece in pieces:
-        nc.vector.scalar_tensor_tensor(
-            wrapped[:, piece], turns[:, piece], -TWO_PI, angle[:, piece], ALU.mult, ALU.add
-        )
-    return wrapped
-
-
-def sin_of_half(nc, result, wrapped, width, shift):
-    for first in range(0, width, PIECE):
-        piece = slice(first, first + PIECE)
-        if shift is None:
-            nc.scalar.activation(result[:, piece], wrapped[:, piece], FUNC.Sin, scale=0.5)
-        else:
-            nc.scalar.activation(result[:, piece], wrapped[:, piece], FUNC.Sin, bias=shift[:], scale=0.5)
 
 
 def tile_jointmembership_fuzzylayer_jaffe_nopool_kernel(tc, x, y, theta, offs, out):
@@ -53,21 +28,19 @@ def tile_jointmembership_fuzzylayer_jaffe_nopool_kernel(tc, x, y, theta, offs, o
         nc.sync.dma_start(offsets[:], offs)
         theta_all = held.tile([IMAGES, CLASSES], F32, name="theta_all")
         nc.sync.dma_start(theta_all[:], theta.broadcast_to([IMAGES, CLASSES]))
-        y_wrapped = wrap_angle(nc, held, y_in, PAIRS, "y")
-        x_wrapped = wrap_angle(nc, held, x_in, PIXELS, "x")
-        theta_wrapped = wrap_angle(nc, held, theta_all, CLASSES, "theta")
 
         sb = held.tile([IMAGES, PAIRS], F32, name="sb")
-        sin_of_half(nc, sb, y_wrapped, PAIRS, None)
+        nc.scalar.activation(sb[:], y_in[:], FUNC.Sin, scale=0.5)
+        cb = held.tile([IMAGES, PAIRS], F32, name="cb")
+        nc.scalar.activation(cb[:], y_in[:], FUNC.Sin, bias=half_pi[:], scale=0.5)
+
         sa_all = held.tile([IMAGES, PIXELS], F32, name="sa_all")
-        sin_of_half(nc, sa_all, x_wrapped, PIXELS, None)
+        nc.scalar.activation(sa_all[:], x_in[:], FUNC.Sin, scale=0.5)
         amp2 = held.tile([IMAGES, PAIRS], F32, name="amp2")
         nc.vector.tensor_tensor(amp2[:], sa_all[:].indirect(offsets[:]), sb[:], ALU.mult)
 
-        cb = held.tile([IMAGES, PAIRS], F32, name="cb")
-        sin_of_half(nc, cb, y_wrapped, PAIRS, half_pi)
         ca_all = held.tile([IMAGES, PIXELS], F32, name="ca_all")
-        sin_of_half(nc, ca_all, x_wrapped, PIXELS, half_pi)
+        nc.scalar.activation(ca_all[:], x_in[:], FUNC.Sin, bias=half_pi[:], scale=0.5)
         amp2_squared = held.tile([IMAGES, PAIRS], F32, name="amp2_squared")
         nc.scalar.activation(amp2_squared[:], amp2[:], FUNC.Square)
 
@@ -86,9 +59,9 @@ def tile_jointmembership_fuzzylayer_jaffe_nopool_kernel(tc, x, y, theta, offs, o
             nc.sync.dma_start(out[:, (2 * t + 1) * PAIRS : (2 * t + 2) * PAIRS], odd_block[:])
 
         sin_theta = held.tile([IMAGES, CLASSES], F32, name="sin_theta")
-        nc.scalar.activation(sin_theta[:], theta_wrapped[:], FUNC.Sin)
+        nc.scalar.activation(sin_theta[:], theta_all[:], FUNC.Sin)
         st = held.tile([IMAGES, CLASSES], F32, name="st")
-        nc.scalar.activation(st[:], theta_wrapped[:], FUNC.Sin, scale=0.5)
+        nc.scalar.activation(st[:], theta_all[:], FUNC.Sin, scale=0.5)
         minus_2_sin_theta = held.tile([IMAGES, CLASSES], F32, name="minus_2_sin_theta")
         nc.vector.tensor_scalar(minus_2_sin_theta[:], sin_theta[:], -2.0, None, ALU.mult)
         st_squared = held.tile([IMAGES, CLASSES], F32, name="st_squared")

@@ -11,7 +11,12 @@ IMAGES = 128
 PIXELS = 1024
 PAIRS = 512
 CLASSES = 7
+PIECE = 256
 HALF = PAIRS // 2
+
+
+def pieces_of(width):
+    return [slice(first, first + PIECE) for first in range(0, width, PIECE)]
 
 
 def tile_jointmembership_fuzzylayer_jaffe_nopool_kernel(tc, x, y, theta, offs, out):
@@ -21,21 +26,26 @@ def tile_jointmembership_fuzzylayer_jaffe_nopool_kernel(tc, x, y, theta, offs, o
         nc.vector.memset(half_pi[:], 0.5 * math.pi)
 
         y_in = held.tile([IMAGES, PAIRS], F32, name="y_in")
-        nc.sync.dma_start(y_in[:], y)
+        for piece in pieces_of(PAIRS):
+            nc.sync.dma_start(y_in[:, piece], y[:, piece])
         x_in = held.tile([IMAGES, PIXELS], F32, name="x_in")
-        nc.sync.dma_start(x_in[:], x)
+        for piece in pieces_of(PIXELS):
+            nc.sync.dma_start(x_in[:, piece], x[:, piece])
         offsets = held.tile([IMAGES, PAIRS // 16], U16, name="offsets")
         nc.sync.dma_start(offsets[:], offs)
         theta_all = held.tile([IMAGES, CLASSES], F32, name="theta_all")
         nc.sync.dma_start(theta_all[:], theta.broadcast_to([IMAGES, CLASSES]))
 
         sb = held.tile([IMAGES, PAIRS], F32, name="sb")
-        nc.scalar.activation(sb[:], y_in[:], FUNC.Sin, scale=0.5)
         cb = held.tile([IMAGES, PAIRS], F32, name="cb")
-        nc.scalar.activation(cb[:], y_in[:], FUNC.Sin, bias=half_pi[:], scale=0.5)
-
+        for piece in pieces_of(PAIRS):
+            nc.scalar.activation(sb[:, piece], y_in[:, piece], FUNC.Sin, scale=0.5)
+            nc.scalar.activation(cb[:, piece], y_in[:, piece], FUNC.Sin, bias=half_pi[:], scale=0.5)
+        sb_squared = held.tile([IMAGES, PAIRS], F32, name="sb_squared")
+        nc.vector.tensor_tensor(sb_squared[:], sb[:], sb[:], ALU.mult)
         sa_all = held.tile([IMAGES, PIXELS], F32, name="sa_all")
-        nc.scalar.activation(sa_all[:], x_in[:], FUNC.Sin, scale=0.5)
+        for piece in pieces_of(PIXELS):
+            nc.scalar.activation(sa_all[:, piece], x_in[:, piece], FUNC.Sin, scale=0.5)
         amp2 = held.tile([IMAGES, PAIRS], F32, name="amp2")
         nc.vector.tensor_tensor(amp2[:], sa_all[:].indirect(offsets[:]), sb[:], ALU.mult)
 
@@ -69,8 +79,6 @@ def tile_jointmembership_fuzzylayer_jaffe_nopool_kernel(tc, x, y, theta, offs, o
         cos_theta = held.tile([IMAGES, CLASSES], F32, name="cos_theta")
         nc.vector.tensor_scalar(cos_theta[:], st_squared[:], -2.0, 1.0, ALU.mult, ALU.add)
 
-        sb_squared = held.tile([IMAGES, PAIRS], F32, name="sb_squared")
-        nc.scalar.activation(sb_squared[:], sb[:], FUNC.Square)
         amp1_squared = held.tile([IMAGES, PAIRS], F32, name="amp1_squared")
         nc.vector.tensor_tensor(amp1_squared[:], sb_squared[:], amp2_squared[:], ALU.subtract)
         ca_squared = held.tile([IMAGES, PAIRS], F32, name="ca_squared")

@@ -37,10 +37,8 @@ def tile_jointmembership_fuzzylayer_jaffe_nopool_kernel(tc, x, y, theta, offs, o
         nc.sync.dma_start(theta_all[:], theta.broadcast_to([IMAGES, CLASSES]))
 
         sb = held.tile([IMAGES, PAIRS], F32, name="sb")
-        cb = held.tile([IMAGES, PAIRS], F32, name="cb")
         for piece in pieces_of(PAIRS):
             nc.scalar.activation(sb[:, piece], y_in[:, piece], FUNC.Sin, scale=0.5)
-            nc.scalar.activation(cb[:, piece], y_in[:, piece], FUNC.Sin, bias=half_pi[:], scale=0.5)
         sb_squared = held.tile([IMAGES, PAIRS], F32, name="sb_squared")
         nc.vector.tensor_tensor(sb_squared[:], sb[:], sb[:], ALU.mult)
         sa_all = held.tile([IMAGES, PIXELS], F32, name="sa_all")
@@ -51,16 +49,21 @@ def tile_jointmembership_fuzzylayer_jaffe_nopool_kernel(tc, x, y, theta, offs, o
 
         ca_all = held.tile([IMAGES, PIXELS], F32, name="ca_all")
         nc.scalar.activation(ca_all[:], x_in[:], FUNC.Sin, bias=half_pi[:], scale=0.5)
+
+        cb = held.tile([IMAGES, PAIRS], F32, name="cb")
+        amp0 = held.tile([IMAGES, PAIRS], F32, name="amp0")
+        for h in range(2):
+            half = slice(h * HALF, (h + 1) * HALF)
+            half_of_list = offsets[:, h * HALF // 16 : (h + 1) * HALF // 16]
+            nc.scalar.activation(cb[:, half], y_in[:, half], FUNC.Sin, bias=half_pi[:], scale=0.5)
+            nc.vector.tensor_tensor(amp0[:, half], ca_all[:].indirect(half_of_list), cb[:, half], ALU.mult)
+
         amp2_squared = held.tile([IMAGES, PAIRS], F32, name="amp2_squared")
         nc.scalar.activation(amp2_squared[:], amp2[:], FUNC.Square)
-
-        amp0 = held.tile([IMAGES, PAIRS], F32, name="amp0")
         amp0_squared = held.tile([IMAGES, PAIRS], F32, name="amp0_squared")
         odd_block = held.tile([IMAGES, PAIRS], F32, name="odd_block")
         for h in range(2):
             half = slice(h * HALF, (h + 1) * HALF)
-            half_of_list = offsets[:, h * HALF // 16 : (h + 1) * HALF // 16]
-            nc.vector.tensor_tensor(amp0[:, half], ca_all[:].indirect(half_of_list), cb[:, half], ALU.mult)
             nc.scalar.activation(amp0_squared[:, half], amp0[:, half], FUNC.Square)
         for h in range(2):
             half = slice(h * HALF, (h + 1) * HALF)

@@ -13,6 +13,7 @@ PAIRS = 512
 CLASSES = 7
 PIECE = 256
 HALF = PAIRS // 2
+ALONE = 5
 
 
 def pieces_of(width):
@@ -68,8 +69,11 @@ def tile_jointmembership_fuzzylayer_jaffe_nopool_kernel(tc, x, y, theta, offs, o
         for h in range(2):
             half = slice(h * HALF, (h + 1) * HALF)
             nc.vector.tensor_tensor(odd_block[:, half], amp0_squared[:, half], amp2_squared[:, half], ALU.add)
-        for t in range(CLASSES):
+        for t in range(ALONE):
             nc.sync.dma_start(out[:, (2 * t + 1) * PAIRS : (2 * t + 2) * PAIRS], odd_block[:])
+        both_blocks = [held.tile([IMAGES, 2 * PAIRS], F32, name=f"both_blocks{t}") for t in range(CLASSES)]
+        for t in range(ALONE, CLASSES):
+            nc.scalar.activation(both_blocks[t][:, PAIRS : 2 * PAIRS], odd_block[:], FUNC.Identity)
 
         sin_theta = held.tile([IMAGES, CLASSES], F32, name="sin_theta")
         nc.scalar.activation(sin_theta[:], theta_all[:], FUNC.Sin)
@@ -94,8 +98,8 @@ def tile_jointmembership_fuzzylayer_jaffe_nopool_kernel(tc, x, y, theta, offs, o
                 ca_term[:], ca_squared[:], FUNC.Identity,
                 bias=st_squared[:, t : t + 1], scale=cos_theta[:, t : t + 1],
             )
-            even_block = held.tile([IMAGES, PAIRS], F32, name=f"even_block{t}")
             nc.vector.scalar_tensor_tensor(
-                even_block[:], amp0_amp2[:], minus_2_sin_theta[:, t : t + 1], ca_term[:], ALU.mult, ALU.add
+                both_blocks[t][:, 0:PAIRS], amp0_amp2[:], minus_2_sin_theta[:, t : t + 1], ca_term[:], ALU.mult, ALU.add
             )
-            nc.sync.dma_start(out[:, 2 * t * PAIRS : (2 * t + 1) * PAIRS], even_block[:])
+            stored = PAIRS if t < ALONE else 2 * PAIRS
+            nc.sync.dma_start(out[:, 2 * t * PAIRS : 2 * t * PAIRS + stored], both_blocks[t][:, 0:stored])

@@ -69,8 +69,10 @@ def tile_jointmembership_fuzzylayer_jaffe_nopool_kernel(tc, x, y, theta, offs, o
         for h in range(2):
             half = slice(h * HALF, (h + 1) * HALF)
             nc.vector.tensor_tensor(odd_block[:, half], amp0_squared[:, half], amp2_squared[:, half], ALU.add)
-        for t in range(ALONE):
-            nc.sync.dma_start(out[:, (2 * t + 1) * PAIRS : (2 * t + 2) * PAIRS], odd_block[:])
+        blocks = out.rearrange("c (b j) -> c b j", j=PAIRS)
+        nc.sync.dma_start(
+            blocks[:, 1 : 2 * ALONE : 2, :], odd_block[:].unsqueeze(1).to_broadcast([IMAGES, ALONE, PAIRS])
+        )
         both_blocks = [held.tile([IMAGES, 2 * PAIRS], F32, name=f"both_blocks{t}") for t in range(CLASSES)]
         for t in range(ALONE, CLASSES):
             nc.scalar.activation(both_blocks[t][:, PAIRS : 2 * PAIRS], odd_block[:], FUNC.Identity)

@@ -13,7 +13,8 @@ PAIRS = 512
 CLASSES = 7
 PIECE = 256
 HALF = PAIRS // 2
-ALONE = 5
+ALONE = [range(0, 3), range(4, CLASSES, 2)]
+RUNS = [(0,), (1,), (2,), (3, 4), (5, 6)]
 
 
 def pieces_of(width):
@@ -70,12 +71,15 @@ def tile_jointmembership_fuzzylayer_jaffe_nopool_kernel(tc, x, y, theta, offs, o
             half = slice(h * HALF, (h + 1) * HALF)
             nc.vector.tensor_tensor(odd_block[:, half], amp0_squared[:, half], amp2_squared[:, half], ALU.add)
         blocks = out.rearrange("c (b j) -> c b j", j=PAIRS)
-        nc.sync.dma_start(
-            blocks[:, 1 : 2 * ALONE : 2, :], odd_block[:].unsqueeze(1).to_broadcast([IMAGES, ALONE, PAIRS])
-        )
-        both_blocks = [held.tile([IMAGES, 2 * PAIRS], F32, name=f"both_blocks{t}") for t in range(CLASSES)]
-        for t in range(ALONE, CLASSES):
-            nc.scalar.activation(both_blocks[t][:, PAIRS : 2 * PAIRS], odd_block[:], FUNC.Identity)
+        for classes in ALONE:
+            nc.sync.dma_start(
+                blocks[:, 2 * classes.start + 1 : 2 * classes.stop : 2 * classes.step, :],
+                odd_block[:].unsqueeze(1).to_broadcast([IMAGES, len(classes), PAIRS]),
+            )
+        runs = [held.tile([IMAGES, 2 * len(run) - 1, PAIRS], F32, name=f"run{run[0]}") for run in RUNS]
+        for run, run_tile in zip(RUNS, runs):
+            if len(run) == 2:
+                nc.scalar.activation(run_tile[:, 1, :], odd_block[:], FUNC.Identity)
 
         sin_theta = held.tile([IMAGES, CLASSES], F32, name="sin_theta")
         nc.scalar.activation(sin_theta[:], theta_all[:], FUNC.Sin)
@@ -94,14 +98,14 @@ def tile_jointmembership_fuzzylayer_jaffe_nopool_kernel(tc, x, y, theta, offs, o
         nc.vector.tensor_tensor(ca_squared[:], amp0_squared[:], amp1_squared[:], ALU.add)
         amp0_amp2 = held.tile([IMAGES, PAIRS], F32, name="amp0_amp2")
         nc.vector.tensor_tensor(amp0_amp2[:], amp0[:], amp2[:], ALU.mult)
-        for t in range(CLASSES):
-            ca_term = held.tile([IMAGES, PAIRS], F32, name=f"ca_term{t}")
-            nc.scalar.activation(
-                ca_term[:], ca_squared[:], FUNC.Identity,
-                bias=st_squared[:, t : t + 1], scale=cos_theta[:, t : t + 1],
-            )
-            nc.vector.scalar_tensor_tensor(
-                both_blocks[t][:, 0:PAIRS], amp0_amp2[:], minus_2_sin_theta[:, t : t + 1], ca_term[:], ALU.mult, ALU.add
-            )
-            stored = PAIRS if t < ALONE else 2 * PAIRS
-            nc.sync.dma_start(out[:, 2 * t * PAIRS : 2 * t * PAIRS + stored], both_blocks[t][:, 0:stored])
+        for run, run_tile in zip(RUNS, runs):
+            for place, t in enumerate(run):
+                ca_term = held.tile([IMAGES, PAIRS], F32, name=f"ca_term{t}")
+                nc.scalar.activation(
+                    ca_term[:], ca_squared[:], FUNC.Identity,
+                    bias=st_squared[:, t : t + 1], scale=cos_theta[:, t : t + 1],
+                )
+                nc.vector.scalar_tensor_tensor(
+                    run_tile[:, 2 * place, :], amp0_amp2[:], minus_2_sin_theta[:, t : t + 1], ca_term[:], ALU.mult, ALU.add
+                )
+            nc.sync.dma_start(blocks[:, 2 * run[0] : 2 * run[-1] + 1, :], run_tile[:])

@@ -14,7 +14,7 @@ CLASSES = 7
 PIECE = 256
 HALF = PAIRS // 2
 ALONE = [range(0, 3), range(4, CLASSES, 2)]
-RUNS = [(0,), (1,), (2,), (3, 4), (5, 6)]
+RUNS = [(0,), (3, 4), (5, 6), (1,), (2,)]
 
 
 def pieces_of(width):

@@ -101,10 +101,15 @@ def tile_jointmembership_fuzzylayer_jaffe_nopool_kernel(tc, x, y, theta, offs, o
         for run, run_tile in zip(RUNS, runs):
             for place, t in enumerate(run):
                 ca_term = held.tile([IMAGES, PAIRS], F32, name=f"ca_term{t}")
-                nc.scalar.activation(
-                    ca_term[:], ca_squared[:], FUNC.Identity,
-                    bias=st_squared[:, t : t + 1], scale=cos_theta[:, t : t + 1],
-                )
+                if run is RUNS[0]:
+                    nc.vector.tensor_scalar(
+                        ca_term[:], ca_squared[:], cos_theta[:, t : t + 1], st_squared[:, t : t + 1], ALU.mult, ALU.add
+                    )
+                else:
+                    nc.scalar.activation(
+                        ca_term[:], ca_squared[:], FUNC.Identity,
+                        bias=st_squared[:, t : t + 1], scale=cos_theta[:, t : t + 1],
+                    )
                 nc.vector.scalar_tensor_tensor(
                     run_tile[:, 2 * place, :], amp0_amp2[:], minus_2_sin_theta[:, t : t + 1], ca_term[:], ALU.mult, ALU.add
                 )

@@ -12,13 +12,11 @@ PIXELS = 1024
 PAIRS = 512
 CLASSES = 7
 PIECE = 256
-HALF = PAIRS // 2
+X_PIECES = [slice(first, first + PIECE) for first in range(0, PIXELS, PIECE)]
+HALVES = [slice(0, PAIRS // 2), slice(PAIRS // 2, PAIRS)]
+QUARTERS = [slice(0, PAIRS // 4), slice(PAIRS // 4, PAIRS // 2)]
 ALONE = [range(0, 3), range(4, CLASSES, 2)]
 RUNS = [(0,), (3, 4), (5, 6), (1,), (2,)]
-
-
-def pieces_of(width):
-    return [slice(first, first + PIECE) for first in range(0, width, PIECE)]
 
 
 def tile_jointmembership_fuzzylayer_jaffe_nopool_kernel(tc, x, y, theta, offs, out):
@@ -28,48 +26,60 @@ def tile_jointmembership_fuzzylayer_jaffe_nopool_kernel(tc, x, y, theta, offs, o
         nc.vector.memset(half_pi[:], 0.5 * math.pi)
 
         y_in = held.tile([IMAGES, PAIRS], F32, name="y_in")
-        for piece in pieces_of(PAIRS):
-            nc.sync.dma_start(y_in[:, piece], y[:, piece])
+        nc.sync.dma_start(y_in[:, HALVES[0]], y[:, HALVES[0]])
         x_in = held.tile([IMAGES, PIXELS], F32, name="x_in")
-        for piece in pieces_of(PIXELS):
+        for piece in X_PIECES:
             nc.sync.dma_start(x_in[:, piece], x[:, piece])
+        nc.sync.dma_start(y_in[:, HALVES[1]], y[:, HALVES[1]])
         offsets = held.tile([IMAGES, PAIRS // 16], U16, name="offsets")
         nc.sync.dma_start(offsets[:], offs)
         theta_all = held.tile([IMAGES, CLASSES], F32, name="theta_all")
         nc.sync.dma_start(theta_all[:], theta.broadcast_to([IMAGES, CLASSES]))
 
         sb = held.tile([IMAGES, PAIRS], F32, name="sb")
-        for piece in pieces_of(PAIRS):
-            nc.scalar.activation(sb[:, piece], y_in[:, piece], FUNC.Sin, scale=0.5)
-        sb_squared = held.tile([IMAGES, PAIRS], F32, name="sb_squared")
-        nc.vector.tensor_tensor(sb_squared[:], sb[:], sb[:], ALU.mult)
-        sa_all = held.tile([IMAGES, PIXELS], F32, name="sa_all")
-        for piece in pieces_of(PIXELS):
-            nc.scalar.activation(sa_all[:, piece], x_in[:, piece], FUNC.Sin, scale=0.5)
-        amp2 = held.tile([IMAGES, PAIRS], F32, name="amp2")
-        nc.vector.tensor_tensor(amp2[:], sa_all[:].indirect(offsets[:]), sb[:], ALU.mult)
-
-        ca_all = held.tile([IMAGES, PIXELS], F32, name="ca_all")
-        nc.scalar.activation(ca_all[:], x_in[:], FUNC.Sin, bias=half_pi[:], scale=0.5)
-
         cb = held.tile([IMAGES, PAIRS], F32, name="cb")
+        sa_all = held.tile([IMAGES, PIXELS], F32, name="sa_all")
+        ca_all = held.tile([IMAGES, PIXELS], F32, name="ca_all")
+        nc.scalar.activation(sb[:, HALVES[0]], y_in[:, HALVES[0]], FUNC.Sin, scale=0.5)
+        for piece in X_PIECES:
+            nc.scalar.activation(sa_all[:, piece], x_in[:, piece], FUNC.Sin, scale=0.5)
+        nc.scalar.activation(sb[:, HALVES[1]], y_in[:, HALVES[1]], FUNC.Sin, scale=0.5)
+        for piece in X_PIECES:
+            nc.scalar.activation(ca_all[:, piece], x_in[:, piece], FUNC.Sin, bias=half_pi[:], scale=0.5)
+        nc.scalar.activation(cb[:, HALVES[1]], y_in[:, HALVES[1]], FUNC.Sin, bias=half_pi[:], scale=0.5)
+
+        w = held.tile([IMAGES, PAIRS // 2], F32, name="w")
+        series = held.tile([IMAGES, PAIRS // 2], F32, name="series")
+        series_times_90 = held.tile([IMAGES, PAIRS // 2], F32, name="series_times_90")
+        for piece in QUARTERS:
+            nc.vector.scalar_tensor_tensor(w[:, piece], y_in[:, piece], -0.125, y_in[:, piece], ALU.mult, ALU.mult)
+        for piece in QUARTERS:
+            nc.vector.scalar_tensor_tensor(series[:, piece], w[:, piece], 15.0, w[:, piece], ALU.add, ALU.mult)
+        for piece in QUARTERS:
+            nc.vector.scalar_tensor_tensor(series_times_90[:, piece], series[:, piece], 90.0, w[:, piece], ALU.add, ALU.mult)
+        for piece in QUARTERS:
+            nc.vector.tensor_scalar(cb[:, piece], series_times_90[:, piece], 1.0 / 90.0, 1.0, ALU.mult, ALU.add)
+
+        amp2 = held.tile([IMAGES, PAIRS], F32, name="amp2")
         amp0 = held.tile([IMAGES, PAIRS], F32, name="amp0")
-        for h in range(2):
-            half = slice(h * HALF, (h + 1) * HALF)
-            half_of_list = offsets[:, h * HALF // 16 : (h + 1) * HALF // 16]
-            nc.scalar.activation(cb[:, half], y_in[:, half], FUNC.Sin, bias=half_pi[:], scale=0.5)
-            nc.vector.tensor_tensor(amp0[:, half], ca_all[:].indirect(half_of_list), cb[:, half], ALU.mult)
+        for amplitude, window, factor in ((amp2, sa_all, sb), (amp0, ca_all, cb)):
+            for half in HALVES:
+                half_of_list = offsets[:, half.start // 16 : half.stop // 16]
+                nc.vector.tensor_tensor(amplitude[:, half], window[:].indirect(half_of_list), factor[:, half], ALU.mult)
 
         amp2_squared = held.tile([IMAGES, PAIRS], F32, name="amp2_squared")
-        nc.scalar.activation(amp2_squared[:], amp2[:], FUNC.Square)
+        for half in HALVES:
+            nc.scalar.activation(amp2_squared[:, half], amp2[:, half], FUNC.Square)
         amp0_squared = held.tile([IMAGES, PAIRS], F32, name="amp0_squared")
-        odd_block = held.tile([IMAGES, PAIRS], F32, name="odd_block")
-        for h in range(2):
-            half = slice(h * HALF, (h + 1) * HALF)
+        sb_squared = sb
+        for half in HALVES:
             nc.scalar.activation(amp0_squared[:, half], amp0[:, half], FUNC.Square)
-        for h in range(2):
-            half = slice(h * HALF, (h + 1) * HALF)
+            nc.scalar.activation(sb_squared[:, half], sb[:, half], FUNC.Square)
+        odd_block = held.tile([IMAGES, PAIRS], F32, name="odd_block")
+        amp1_squared = held.tile([IMAGES, PAIRS], F32, name="amp1_squared")
+        for half in HALVES:
             nc.vector.tensor_tensor(odd_block[:, half], amp0_squared[:, half], amp2_squared[:, half], ALU.add)
+            nc.vector.tensor_tensor(amp1_squared[:, half], sb_squared[:, half], amp2_squared[:, half], ALU.subtract)
         blocks = out.rearrange("c (b j) -> c b j", j=PAIRS)
         for classes in ALONE:
             nc.sync.dma_start(
@@ -83,21 +93,18 @@ def tile_jointmembership_fuzzylayer_jaffe_nopool_kernel(tc, x, y, theta, offs, o
 
         sin_theta = held.tile([IMAGES, CLASSES], F32, name="sin_theta")
         nc.scalar.activation(sin_theta[:], theta_all[:], FUNC.Sin)
+        cos_theta = held.tile([IMAGES, CLASSES], F32, name="cos_theta")
+        nc.scalar.activation(cos_theta[:], theta_all[:], FUNC.Sin, bias=half_pi[:])
         st = held.tile([IMAGES, CLASSES], F32, name="st")
         nc.scalar.activation(st[:], theta_all[:], FUNC.Sin, scale=0.5)
-        minus_2_sin_theta = held.tile([IMAGES, CLASSES], F32, name="minus_2_sin_theta")
-        nc.vector.tensor_scalar(minus_2_sin_theta[:], sin_theta[:], -2.0, None, ALU.mult)
         st_squared = held.tile([IMAGES, CLASSES], F32, name="st_squared")
-        nc.vector.tensor_tensor(st_squared[:], st[:], st[:], ALU.mult)
-        cos_theta = held.tile([IMAGES, CLASSES], F32, name="cos_theta")
-        nc.vector.tensor_scalar(cos_theta[:], st_squared[:], -2.0, 1.0, ALU.mult, ALU.add)
+        nc.scalar.activation(st_squared[:], st[:], FUNC.Square)
 
-        amp1_squared = held.tile([IMAGES, PAIRS], F32, name="amp1_squared")
-        nc.vector.tensor_tensor(amp1_squared[:], sb_squared[:], amp2_squared[:], ALU.subtract)
         ca_squared = held.tile([IMAGES, PAIRS], F32, name="ca_squared")
-        nc.vector.tensor_tensor(ca_squared[:], amp0_squared[:], amp1_squared[:], ALU.add)
-        amp0_amp2 = held.tile([IMAGES, PAIRS], F32, name="amp0_amp2")
-        nc.vector.tensor_tensor(amp0_amp2[:], amp0[:], amp2[:], ALU.mult)
+        for half in HALVES:
+            nc.vector.tensor_tensor(ca_squared[:, half], amp0_squared[:, half], amp1_squared[:, half], ALU.add)
+        product = sb_squared
+        nc.vector.scalar_tensor_tensor(product[:], amp0[:], -2.0, amp2[:], ALU.mult, ALU.mult)
         for run, run_tile in zip(RUNS, runs):
             for place, t in enumerate(run):
                 ca_term = held.tile([IMAGES, PAIRS], F32, name=f"ca_term{t}")
@@ -111,6 +118,6 @@ def tile_jointmembership_fuzzylayer_jaffe_nopool_kernel(tc, x, y, theta, offs, o
                         bias=st_squared[:, t : t + 1], scale=cos_theta[:, t : t + 1],
                     )
                 nc.vector.scalar_tensor_tensor(
-                    run_tile[:, 2 * place, :], amp0_amp2[:], minus_2_sin_theta[:, t : t + 1], ca_term[:], ALU.mult, ALU.add
+                    run_tile[:, 2 * place, :], product[:], sin_theta[:, t : t + 1], ca_term[:], ALU.mult, ALU.add
                 )
             nc.sync.dma_start(blocks[:, 2 * run[0] : 2 * run[-1] + 1, :], run_tile[:])

@@ -104,14 +104,17 @@ def tile_jointmembership_fuzzylayer_jaffe_nopool_kernel(tc, x, y, theta, offs, o
         for half in HALVES:
             nc.vector.tensor_tensor(ca_squared[:, half], amp0_squared[:, half], amp1_squared[:, half], ALU.add)
         product = sb_squared
-        nc.vector.scalar_tensor_tensor(product[:], amp0[:], -2.0, amp2[:], ALU.mult, ALU.mult)
+        for half in HALVES:
+            nc.vector.scalar_tensor_tensor(product[:, half], amp0[:, half], -2.0, amp2[:, half], ALU.mult, ALU.mult)
         for run, run_tile in zip(RUNS, runs):
             for place, t in enumerate(run):
                 ca_term = held.tile([IMAGES, PAIRS], F32, name=f"ca_term{t}")
                 if run is RUNS[0]:
-                    nc.vector.tensor_scalar(
-                        ca_term[:], ca_squared[:], cos_theta[:, t : t + 1], st_squared[:, t : t + 1], ALU.mult, ALU.add
-                    )
+                    for half in HALVES:
+                        nc.vector.tensor_scalar(
+                            ca_term[:, half], ca_squared[:, half],
+                            cos_theta[:, t : t + 1], st_squared[:, t : t + 1], ALU.mult, ALU.add,
+                        )
                 else:
                     nc.scalar.activation(
                         ca_term[:], ca_squared[:], FUNC.Identity,

@@ -14,9 +14,10 @@ CLASSES = 7
 PIECE = 256
 X_PIECES = [slice(first, first + PIECE) for first in range(0, PIXELS, PIECE)]
 HALVES = [slice(0, PAIRS // 2), slice(PAIRS // 2, PAIRS)]
+PARTS = [slice(0, 256), slice(256, 384), slice(384, PAIRS)]
 QUARTERS = [slice(0, PAIRS // 4), slice(PAIRS // 4, PAIRS // 2)]
 ALONE = [range(0, 3), range(4, CLASSES, 2)]
-RUNS = [(0,), (3, 4), (5, 6), (1,), (2,)]
+RUNS = [(0,), (6, 7), (8,), (10, 11, 12), (2,), (4,)]
 
 
 def tile_jointmembership_fuzzylayer_jaffe_nopool_kernel(tc, x, y, theta, offs, out):
@@ -62,23 +63,26 @@ def tile_jointmembership_fuzzylayer_jaffe_nopool_kernel(tc, x, y, theta, offs, o
 
         amp2 = held.tile([IMAGES, PAIRS], F32, name="amp2")
         amp0 = held.tile([IMAGES, PAIRS], F32, name="amp0")
-        for amplitude, window, factor in ((amp2, sa_all, sb), (amp0, ca_all, cb)):
-            for half in HALVES:
-                half_of_list = offsets[:, half.start // 16 : half.stop // 16]
-                nc.vector.tensor_tensor(amplitude[:, half], window[:].indirect(half_of_list), factor[:, half], ALU.mult)
+        for amplitude, window, factor, parts in ((amp2, sa_all, sb, HALVES), (amp0, ca_all, cb, PARTS)):
+            for part in parts:
+                part_of_list = offsets[:, part.start // 16 : part.stop // 16]
+                nc.vector.tensor_tensor(amplitude[:, part], window[:].indirect(part_of_list), factor[:, part], ALU.mult)
 
         amp2_squared = held.tile([IMAGES, PAIRS], F32, name="amp2_squared")
         for half in HALVES:
             nc.scalar.activation(amp2_squared[:, half], amp2[:, half], FUNC.Square)
         amp0_squared = held.tile([IMAGES, PAIRS], F32, name="amp0_squared")
         sb_squared = sb
-        for half in HALVES:
-            nc.scalar.activation(amp0_squared[:, half], amp0[:, half], FUNC.Square)
-            nc.scalar.activation(sb_squared[:, half], sb[:, half], FUNC.Square)
+        nc.scalar.activation(amp0_squared[:, PARTS[0]], amp0[:, PARTS[0]], FUNC.Square)
+        nc.scalar.activation(sb_squared[:, HALVES[0]], sb[:, HALVES[0]], FUNC.Square)
+        for part in PARTS[1:]:
+            nc.scalar.activation(amp0_squared[:, part], amp0[:, part], FUNC.Square)
+        nc.scalar.activation(sb_squared[:, HALVES[1]], sb[:, HALVES[1]], FUNC.Square)
         odd_block = held.tile([IMAGES, PAIRS], F32, name="odd_block")
         amp1_squared = held.tile([IMAGES, PAIRS], F32, name="amp1_squared")
-        for half in HALVES:
-            nc.vector.tensor_tensor(odd_block[:, half], amp0_squared[:, half], amp2_squared[:, half], ALU.add)
+        for half, parts in ((HALVES[0], PARTS[:1]), (HALVES[1], PARTS[1:])):
+            for part in parts:
+                nc.vector.tensor_tensor(odd_block[:, part], amp0_squared[:, part], amp2_squared[:, part], ALU.add)
             nc.vector.tensor_tensor(amp1_squared[:, half], sb_squared[:, half], amp2_squared[:, half], ALU.subtract)
         blocks = out.rearrange("c (b j) -> c b j", j=PAIRS)
         for classes in ALONE:
@@ -86,10 +90,11 @@ def tile_jointmembership_fuzzylayer_jaffe_nopool_kernel(tc, x, y, theta, offs, o
                 blocks[:, 2 * classes.start + 1 : 2 * classes.stop : 2 * classes.step, :],
                 odd_block[:].unsqueeze(1).to_broadcast([IMAGES, len(classes), PAIRS]),
             )
-        runs = [held.tile([IMAGES, 2 * len(run) - 1, PAIRS], F32, name=f"run{run[0]}") for run in RUNS]
+        runs = [held.tile([IMAGES, len(run), PAIRS], F32, name=f"run{run[0]}") for run in RUNS]
         for run, run_tile in zip(RUNS, runs):
-            if len(run) == 2:
-                nc.scalar.activation(run_tile[:, 1, :], odd_block[:], FUNC.Identity)
+            for place, block in enumerate(run):
+                if block % 2 == 1:
+                    nc.scalar.activation(run_tile[:, place, :], odd_block[:], FUNC.Identity)
 
         sin_theta = held.tile([IMAGES, CLASSES], F32, name="sin_theta")
         nc.scalar.activation(sin_theta[:], theta_all[:], FUNC.Sin)
@@ -107,7 +112,10 @@ def tile_jointmembership_fuzzylayer_jaffe_nopool_kernel(tc, x, y, theta, offs, o
         for half in HALVES:
             nc.vector.scalar_tensor_tensor(product[:, half], amp0[:, half], -2.0, amp2[:, half], ALU.mult, ALU.mult)
         for run, run_tile in zip(RUNS, runs):
-            for place, t in enumerate(run):
+            for place, block in enumerate(run):
+                if block % 2 == 1:
+                    continue
+                t = block // 2
                 ca_term = held.tile([IMAGES, PAIRS], F32, name=f"ca_term{t}")
                 if run is RUNS[0]:
                     for half in HALVES:
@@ -121,6 +129,6 @@ def tile_jointmembership_fuzzylayer_jaffe_nopool_kernel(tc, x, y, theta, offs, o
                         bias=st_squared[:, t : t + 1], scale=cos_theta[:, t : t + 1],
                     )
                 nc.vector.scalar_tensor_tensor(
-                    run_tile[:, 2 * place, :], product[:], sin_theta[:, t : t + 1], ca_term[:], ALU.mult, ALU.add
+                    run_tile[:, place, :], product[:], sin_theta[:, t : t + 1], ca_term[:], ALU.mult, ALU.add
                 )
-            nc.sync.dma_start(blocks[:, 2 * run[0] : 2 * run[-1] + 1, :], run_tile[:])
+            nc.sync.dma_start(blocks[:, run[0] : run[-1] + 1, :], run_tile[:])

import math

import concourse.mybir as mybir

F32 = mybir.dt.float32
U16 = mybir.dt.uint16
ALU = mybir.AluOpType
FUNC = mybir.ActivationFunctionType

IMAGES = 128
PIXELS = 1024
PAIRS = 512
CLASSES = 7
PIECE = 256
X_PIECES = [slice(first, first + PIECE) for first in range(0, PIXELS, PIECE)]
HALVES = [slice(0, PAIRS // 2), slice(PAIRS // 2, PAIRS)]
PARTS = [slice(0, 256), slice(256, 384), slice(384, PAIRS)]
QUARTERS = [slice(0, PAIRS // 4), slice(PAIRS // 4, PAIRS // 2)]
ALONE = [range(0, 3), range(4, CLASSES, 2)]
RUNS = [(0,), (6, 7), (8,), (10, 11, 12), (2,), (4,)]


def tile_jointmembership_fuzzylayer_jaffe_nopool_kernel(tc, x, y, theta, offs, out):
    nc = tc.nc
    with tc.tile_pool(name="held", bufs=1) as held:
        half_pi = held.tile([IMAGES, 1], F32, name="half_pi")
        nc.vector.memset(half_pi[:], 0.5 * math.pi)

        y_in = held.tile([IMAGES, PAIRS], F32, name="y_in")
        nc.sync.dma_start(y_in[:, HALVES[0]], y[:, HALVES[0]])
        x_in = held.tile([IMAGES, PIXELS], F32, name="x_in")
        for piece in X_PIECES:
            nc.sync.dma_start(x_in[:, piece], x[:, piece])
        nc.sync.dma_start(y_in[:, HALVES[1]], y[:, HALVES[1]])
        offsets = held.tile([IMAGES, PAIRS // 16], U16, name="offsets")
        nc.sync.dma_start(offsets[:], offs)
        theta_all = held.tile([IMAGES, CLASSES], F32, name="theta_all")
        nc.sync.dma_start(theta_all[:], theta.broadcast_to([IMAGES, CLASSES]))

        sb = held.tile([IMAGES, PAIRS], F32, name="sb")
        cb = held.tile([IMAGES, PAIRS], F32, name="cb")
        sa_all = held.tile([IMAGES, PIXELS], F32, name="sa_all")
        ca_all = held.tile([IMAGES, PIXELS], F32, name="ca_all")
        nc.scalar.activation(sb[:, HALVES[0]], y_in[:, HALVES[0]], FUNC.Sin, scale=0.5)
        for piece in X_PIECES:
            nc.scalar.activation(sa_all[:, piece], x_in[:, piece], FUNC.Sin, scale=0.5)
        nc.scalar.activation(sb[:, HALVES[1]], y_in[:, HALVES[1]], FUNC.Sin, scale=0.5)
        for piece in X_PIECES:
            nc.scalar.activation(ca_all[:, piece], x_in[:, piece], FUNC.Sin, bias=half_pi[:], scale=0.5)
        nc.scalar.activation(cb[:, HALVES[1]], y_in[:, HALVES[1]], FUNC.Sin, bias=half_pi[:], scale=0.5)

        w = held.tile([IMAGES, PAIRS // 2], F32, name="w")
        series = held.tile([IMAGES, PAIRS // 2], F32, name="series")
        series_times_90 = held.tile([IMAGES, PAIRS // 2], F32, name="series_times_90")
        for piece in QUARTERS:
            nc.vector.scalar_tensor_tensor(w[:, piece], y_in[:, piece], -0.125, y_in[:, piece], ALU.mult, ALU.mult)
        for piece in QUARTERS:
            nc.vector.scalar_tensor_tensor(series[:, piece], w[:, piece], 15.0, w[:, piece], ALU.add, ALU.mult)
        for piece in QUARTERS:
            nc.vector.scalar_tensor_tensor(series_times_90[:, piece], series[:, piece], 90.0, w[:, piece], ALU.add, ALU.mult)
        for piece in QUARTERS:
            nc.vector.tensor_scalar(cb[:, piece], series_times_90[:, piece], 1.0 / 90.0, 1.0, ALU.mult, ALU.add)

        amp2 = held.tile([IMAGES, PAIRS], F32, name="amp2")
        amp0 = held.tile([IMAGES, PAIRS], F32, name="amp0")
        for amplitude, window, factor, parts in ((amp2, sa_all, sb, HALVES), (amp0, ca_all, cb, PARTS)):
            for part in parts:
                part_of_list = offsets[:, part.start // 16 : part.stop // 16]
                nc.vector.tensor_tensor(amplitude[:, part], window[:].indirect(part_of_list), factor[:, part], ALU.mult)

        amp2_squared = held.tile([IMAGES, PAIRS], F32, name="amp2_squared")
        for half in HALVES:
            nc.scalar.activation(amp2_squared[:, half], amp2[:, half], FUNC.Square)
        amp0_squared = held.tile([IMAGES, PAIRS], F32, name="amp0_squared")
        sb_squared = sb
        nc.scalar.activation(amp0_squared[:, PARTS[0]], amp0[:, PARTS[0]], FUNC.Square)
        nc.scalar.activation(sb_squared[:, HALVES[0]], sb[:, HALVES[0]], FUNC.Square)
        for part in PARTS[1:]:
            nc.scalar.activation(amp0_squared[:, part], amp0[:, part], FUNC.Square)
        nc.scalar.activation(sb_squared[:, HALVES[1]], sb[:, HALVES[1]], FUNC.Square)
        odd_block = held.tile([IMAGES, PAIRS], F32, name="odd_block")
        amp1_squared = held.tile([IMAGES, PAIRS], F32, name="amp1_squared")
        for half, parts in ((HALVES[0], PARTS[:1]), (HALVES[1], PARTS[1:])):
            for part in parts:
                nc.vector.tensor_tensor(odd_block[:, part], amp0_squared[:, part], amp2_squared[:, part], ALU.add)
            nc.vector.tensor_tensor(amp1_squared[:, half], sb_squared[:, half], amp2_squared[:, half], ALU.subtract)
        blocks = out.rearrange("c (b j) -> c b j", j=PAIRS)
        for classes in ALONE:
            nc.sync.dma_start(
                blocks[:, 2 * classes.start + 1 : 2 * classes.stop : 2 * classes.step, :],
                odd_block[:].unsqueeze(1).to_broadcast([IMAGES, len(classes), PAIRS]),
            )
        runs = [held.tile([IMAGES, len(run), PAIRS], F32, name=f"run{run[0]}") for run in RUNS]
        for run, run_tile in zip(RUNS, runs):
            for place, block in enumerate(run):
                if block % 2 == 1:
                    nc.scalar.activation(run_tile[:, place, :], odd_block[:], FUNC.Identity)

        sin_theta = held.tile([IMAGES, CLASSES], F32, name="sin_theta")
        nc.scalar.activation(sin_theta[:], theta_all[:], FUNC.Sin)
        cos_theta = held.tile([IMAGES, CLASSES], F32, name="cos_theta")
        nc.scalar.activation(cos_theta[:], theta_all[:], FUNC.Sin, bias=half_pi[:])
        st = held.tile([IMAGES, CLASSES], F32, name="st")
        nc.scalar.activation(st[:], theta_all[:], FUNC.Sin, scale=0.5)
        st_squared = held.tile([IMAGES, CLASSES], F32, name="st_squared")
        nc.scalar.activation(st_squared[:], st[:], FUNC.Square)

        ca_squared = held.tile([IMAGES, PAIRS], F32, name="ca_squared")
        for half in HALVES:
            nc.vector.tensor_tensor(ca_squared[:, half], amp0_squared[:, half], amp1_squared[:, half], ALU.add)
        product = sb_squared
        for half in HALVES:
            nc.vector.scalar_tensor_tensor(product[:, half], amp0[:, half], -2.0, amp2[:, half], ALU.mult, ALU.mult)
        for run, run_tile in zip(RUNS, runs):
            for place, block in enumerate(run):
                if block % 2 == 1:
                    continue
                t = block // 2
                ca_term = held.tile([IMAGES, PAIRS], F32, name=f"ca_term{t}")
                if run is RUNS[0]:
                    for half in HALVES:
                        nc.vector.tensor_scalar(
                            ca_term[:, half], ca_squared[:, half],
                            cos_theta[:, t : t + 1], st_squared[:, t : t + 1], ALU.mult, ALU.add,
                        )
                else:
                    nc.scalar.activation(
                        ca_term[:], ca_squared[:], FUNC.Identity,
                        bias=st_squared[:, t : t + 1], scale=cos_theta[:, t : t + 1],
                    )
                nc.vector.scalar_tensor_tensor(
                    run_tile[:, place, :], product[:], sin_theta[:, t : t + 1], ca_term[:], ALU.mult, ALU.add
                )
            nc.sync.dma_start(blocks[:, run[0] : run[-1] + 1, :], run_tile[:])
